import numpy as np
import ml_dtypes


def mxq(x, axis, fmt="e4m3"):
    dtype, down = {"e4m3": (ml_dtypes.float8_e4m3fn, 7), "e5m2": (ml_dtypes.float8_e5m2, 14)}[fmt]
    v = np.moveaxis(np.asarray(x, np.float32).astype(ml_dtypes.bfloat16).astype(np.float64), axis, -1)
    blocks = v.reshape(v.shape[:-1] + (-1, 32))
    amax = np.abs(blocks).max(-1, keepdims=True)
    byte = np.maximum(np.where(amax > 0, np.frexp(amax)[1] - 1 + 127, 0) - down, 1)
    scale = np.exp2(byte - 127.0)
    codes = (blocks / scale).astype(np.float32).astype(dtype).astype(np.float64)
    return np.moveaxis((codes * scale).reshape(v.shape), -1, axis)


WIDE = False


def mx_kscale(k):
    if not WIDE:
        return np.ones(k)
    levels = np.array([10, -10, 5, -5, 0])
    if k % 512:
        return np.exp2(np.random.permutation(np.resize(levels, k // 32))).repeat(32)
    a = np.empty((k // 512, 16))
    for p in range(k // 512):
        a[p, :8] = np.random.permutation(np.resize(levels, 8))
        for g in range(8):
            far = levels[np.abs(levels - a[p, g]) >= 10]
            a[p, g + 8] = far[np.random.randint(len(far))]
    return np.exp2(a.ravel()).repeat(32)


BF16 = ml_dtypes.bfloat16


def bf(x):
    return np.asarray(x, np.float32).astype(BF16)


def f64(x):
    return np.asarray(x).astype(np.float64)


B, T, D, H, DH, DFF = 4, 256, 1024, 16, 64, 4096
HD = H * DH
EPS = 1e-5


def layer_norm(x, w):
    mu = x.mean(-1, keepdims=True)
    var = ((x - mu) ** 2).mean(-1, keepdims=True)
    return (x - mu) * (1.0 / np.sqrt(var + EPS)) * w


def setup_inputs():
    s = mx_kscale(D)
    spread = 0.5 + np.random.random((B, T, 1))
    shift = 0.5 * np.random.standard_normal((B, T, 1))
    return {"x": bf(np.random.standard_normal((B, T, D)) * spread + shift),
            "ln1_w": bf((1.0 + 0.1 * np.random.standard_normal(D)) * s),
            "qkv_w": bf(np.random.standard_normal((3 * HD, D)) / np.sqrt(D) / s[None, :])}


def reference(x, ln1_w, qkv_w):
    h = layer_norm(f64(x), f64(ln1_w))
    qkv = mxq(h, 2, "e4m3") @ mxq(f64(qkv_w), 1, "e4m3").T
    qkv = qkv.reshape(B, T, 3, H, DH)
    q = qkv[:, :, 0].transpose(0, 2, 1, 3)
    k = qkv[:, :, 1].transpose(0, 2, 1, 3)
    v = qkv[:, :, 2].transpose(0, 2, 1, 3)
    return q, k, v

@@ -1,0 +1,251 @@
+from contextlib import ExitStack
+
+import concourse.mybir as mybir
+from concourse.masks import make_identity
+
+F32 = mybir.dt.float32
+BF16 = mybir.dt.bfloat16
+U32 = mybir.dt.uint32
+U8 = mybir.dt.uint8
+FP8X4 = mybir.dt.float8_e4m3fn_x4
+ALU = mybir.AluOpType
+ACT = mybir.ActivationFunctionType
+
+P = 128
+BATCH, SEQ, DIM = 4, 256, 1024
+HEADS, HEAD_DIM = 16, 64
+EPS = 1e-5
+
+PACK = 4
+K_PASS = P * PACK
+PASSES = DIM // K_PASS
+SLOTS = BATCH * SEQ // P
+HALF = SLOTS // 2
+CHUNK = 512
+CHUNK_HEADS = CHUNK // HEAD_DIM
+CHUNKS = 3 * HEADS * HEAD_DIM // CHUNK
+ROW_BLOCKS = CHUNK // P
+BN_WIDTH = 512
+
+EARLY_CHUNKS = HALF
+
+FLOPS = 2 * BATCH * SEQ * DIM * 3 * HEADS * HEAD_DIM
+
+
+def tile_traceableencoderlayer_pa_kernel(tc, x, ln1_w, qkv_w, out_0, out_1, out_2):
+    nc = tc.nc
+    outs = (out_0, out_1, out_2)
+
+    with ExitStack() as ctx:
+        keep = ctx.enter_context(tc.tile_pool(name="keep", bufs=1))
+        small = ctx.enter_context(tc.tile_pool(name="small", bufs=4))
+        stage = ctx.enter_context(tc.tile_pool(name="stage", bufs=2))
+        w_pool = ctx.enter_context(tc.tile_pool(name="w_pool", bufs=CHUNKS))
+        res_pool = ctx.enter_context(tc.tile_pool(name="res_pool", bufs=4))
+        psum = ctx.enter_context(tc.psum_pool(name="psum", bufs=8))
+        ctx.enter_context(tc.manual_schedule())
+
+        x_sb = keep.tile([P, SLOTS, DIM], BF16)
+        w_rows = qkv_w.rearrange("(c a p) k -> c p a k", a=ROW_BLOCKS, p=P)
+        w_raw = []
+
+        def load_tokens(first_slot, n_slots):
+            slots = slice(first_slot, first_slot + n_slots)
+            for b in range(BATCH):
+                nc.sync.dma_start(
+                    out=x_sb[b:P:BATCH, slots, :],
+                    in_=x[b].rearrange("(i r) k -> i r k", r=SLOTS)[:, slots, :],
+                )
+
+        def load_weights(c):
+            raw = w_pool.tile([P, ROW_BLOCKS, DIM], BF16, name="raw")
+            nc.sync.dma_start(out=raw[:], in_=w_rows[c])
+            w_raw.append(raw)
+
+        load_tokens(0, 2)
+        load_tokens(2, 2)
+        load_weights(0)
+        load_tokens(4, 2)
+        load_tokens(6, 2)
+        for c in range(1, CHUNKS):
+            load_weights(c)
+
+        identity = keep.tile([P, P], F32)
+        make_identity(nc, identity[:])
+        minus_half = keep.tile([P, 2], F32)
+        nc.gpsimd.memset(minus_half[:], -0.5)
+        table_warmer = keep.tile([P, 1], F32)
+        nc.scalar.activation(out=table_warmer[:], in_=minus_half[:, 0:1], func=ACT.Identity)
+
+        gain_rows = keep.tile([P, K_PASS], BF16)
+        nc.vector.memset(gain_rows[:], 0.0)
+        nc.scalar.dma_start(
+            out=gain_rows[0:PASSES, :], in_=ln1_w.rearrange("(r c) -> r c", c=K_PASS)
+        )
+        gain_flip = psum.tile([P, PACK, P], F32, tag="bank")
+        for u in range(2):
+            nc.tensor.transpose(
+                gain_flip[:, u, :], gain_rows[:].bitcast(F32)[:, u : 2 * P : 2], identity[:]
+            )
+        gain_words = keep.tile([P, PASSES, 2], F32)
+        gain = keep.tile([P, PASSES, PACK], F32)
+
+        def widen_gain():
+            nc.vector.tensor_copy(
+                out=gain_words[:], in_=gain_flip[:, 0:2, 0:PASSES].rearrange("p u g -> p g u")
+            )
+            nc.vector.tensor_copy(
+                out=gain[:].rearrange("p g j -> p (g j)"),
+                in_=gain_words[:].rearrange("p g u -> p (g u)").bitcast(BF16),
+            )
+
+        mean_var = keep.tile([P, SLOTS, 2], F32)
+        neg_mean = keep.tile([P, SLOTS], F32)
+        var_eps = keep.tile([P, SLOTS], F32)
+        rstd = keep.tile([P, SLOTS], F32)
+        shift = keep.tile([P, SLOTS], F32)
+        h_codes = keep.tile([P, SLOTS, PASSES, P], U32, align_bytes=64)
+        h_scales = keep.tile([P, SLOTS, PASSES, P], U8, align_bytes=64)
+        w_codes = keep.tile([P, CHUNKS, PASSES, CHUNK], U32, align_bytes=64)
+        w_scales = keep.tile([P, CHUNKS, PASSES, CHUNK], U8, align_bytes=64)
+        z_tiles = {}
+        h_grouped_tiles = {}
+        w_grouped_tiles = {}
+
+        def statistics(first_slot):
+            pair = slice(first_slot, first_slot + 2)
+            for r in range(first_slot, first_slot + 2):
+                stats = small.tile([P, DIM // BN_WIDTH, 6], F32)
+                for s in range(DIM // BN_WIDTH):
+                    nc.vector.bn_stats(
+                        out=stats[:, s, :], in_=x_sb[:, r, s * BN_WIDTH : (s + 1) * BN_WIDTH]
+                    )
+                nc.vector.bn_aggr(out=mean_var[:, r, :], in_=stats[:].rearrange("p s f -> p (s f)"))
+            nc.vector.tensor_scalar_mul(out=neg_mean[:, pair], in0=mean_var[:, pair, 0], scalar1=-1.0)
+            nc.gpsimd.tensor_scalar_add(out=var_eps[:, pair], in0=mean_var[:, pair, 1], scalar1=EPS)
+            nc.gpsimd.tensor_tensor(
+                out=rstd[:, pair], in0=var_eps[:, pair], in1=minus_half[:], op=ALU.pow
+            )
+            nc.gpsimd.tensor_tensor(
+                out=shift[:, pair], in0=neg_mean[:, pair], in1=rstd[:, pair], op=ALU.mult
+            )
+
+        def normalise(r):
+            z = stage.tile([P, PASSES, PACK, P], F32, name="z", bufs=4)
+            nc.scalar.activation(
+                out=z[:],
+                in_=x_sb[:, r, :].rearrange("p (g w j) -> p g j w", w=P, j=PACK),
+                func=ACT.Identity,
+                scale=rstd[:, r : r + 1],
+                bias=shift[:, r : r + 1],
+            )
+            z_tiles[r] = z
+
+        def flip_tokens(r):
+            z = z_tiles[r]
+            h_grouped = stage.tile([P, PASSES, P, PACK], BF16, name="h_grouped", align_bytes=64)
+            for g in range(PASSES):
+                z_flip = psum.tile([P, PACK, P], F32, tag="bank")
+                for j in range(PACK):
+                    nc.tensor.transpose(z_flip[:, j, :], z[:, g, j, :], identity[:])
+                nc.vector.tensor_tensor(
+                    out=h_grouped[:, g, :, :],
+                    in0=z_flip[:].rearrange("p j i -> p i j"),
+                    in1=gain[:, g, :].unsqueeze(1).to_broadcast([P, P, PACK]),
+                    op=ALU.mult,
+                )
+            h_grouped_tiles[r] = h_grouped
+
+        def quantise_tokens(r):
+            nc.vector.quantize_mx(
+                out=h_codes[:, r, :, :].rearrange("p g i -> p (g i)").bitcast(FP8X4),
+                scales=h_scales[:, r, :, :].rearrange("p g i -> p (g i)"),
+                in_=h_grouped_tiles[r][:].rearrange("p g i j -> p (g i j)"),
+            )
+
+        def flip_weights(c):
+            words = w_raw[c][:].bitcast(F32)
+            w_grouped = stage.tile([P, PASSES, CHUNK, PACK], BF16, name="w_grouped", align_bytes=64)
+            grouped_words = w_grouped[:].bitcast(F32)
+            for g in range(PASSES):
+                for pair in range(ROW_BLOCKS // 2):
+                    w_flip = psum.tile([P, 2, 2, P], F32, tag="bank")
+                    for u in range(2):
+                        for a in range(2):
+                            nc.tensor.transpose(
+                                w_flip[:, u, a, :],
+                                words[:, 2 * pair + a, 2 * P * g + u : 2 * P * (g + 1) : 2],
+                                identity[:],
+                            )
+                    nc.scalar.copy(
+                        out=grouped_words[:, g, 2 * pair * P : (2 * pair + 2) * P, :],
+                        in_=w_flip[:].rearrange("p u a n -> p (a n) u"),
+                    )
+            w_grouped_tiles[c] = w_grouped
+
+        def quantise_weights(c):
+            nc.vector.quantize_mx(
+                out=w_codes[:, c, :, :].rearrange("p g n -> p (g n)").bitcast(FP8X4),
+                scales=w_scales[:, c, :, :].rearrange("p g n -> p (g n)"),
+                in_=w_grouped_tiles[c][:].rearrange("p g n j -> p (g n j)"),
+            )
+
+        def project(c, first_slot, n_slots):
+            result = res_pool.tile([P, CHUNK_HEADS, n_slots, HEAD_DIM], F32, tag="result")
+            for r in range(first_slot, first_slot + n_slots):
+                acc = psum.tile([P, CHUNK], F32, tag="bank")
+                for g in range(PASSES):
+                    nc.tensor.matmul_mx(
+                        out=acc[:],
+                        lhsT=h_codes[:, r, g, :].bitcast(FP8X4),
+                        lhsT_scale=h_scales[:, r, g, :],
+                        rhs=w_codes[:, c, g, :].bitcast(FP8X4),
+                        rhs_scale=w_scales[:, c, g, :],
+                        start=(g == 0),
+                        stop=(g == PASSES - 1),
+                    )
+                by_head = acc[:].rearrange("p (n d) -> p n d", d=HEAD_DIM)
+                if r % 2 == 0:
+                    nc.scalar.copy(out=result[:, :, r - first_slot, :], in_=by_head)
+                else:
+                    nc.vector.tensor_copy(out=result[:, :, r - first_slot, :], in_=by_head)
+            which, first_head = divmod(c * CHUNK_HEADS, HEADS)
+            for b in range(BATCH):
+                nc.sync.dma_start(
+                    out=outs[which][b, first_head : first_head + CHUNK_HEADS].rearrange(
+                        "n (i r) d -> i n r d", r=SLOTS
+                    )[:, :, first_slot : first_slot + n_slots, :],
+                    in_=result[b:P:BATCH],
+                )
+
+        for first_slot in range(0, SLOTS, 2):
+            statistics(first_slot)
+        widen_gain()
+        flip_weights(0)
+        for r in range(HALF):
+            normalise(r)
+        flip_tokens(0)
+        flip_tokens(1)
+        quantise_tokens(0)
+        quantise_weights(0)
+        for r in range(2, HALF):
+            flip_tokens(r)
+            quantise_tokens(r - 1)
+        quantise_tokens(HALF - 1)
+        flip_weights(1)
+        normalise(HALF)
+        quantise_weights(1)
+
+        for i in range(HALF):
+            flip_weights(i + 2)
+            project(i, 0, HALF)
+            if HALF + i + 1 < SLOTS:
+                normalise(HALF + i + 1)
+            flip_tokens(HALF + i)
+            quantise_tokens(HALF + i)
+            quantise_weights(i + 2)
+
+        for c in range(EARLY_CHUNKS):
+            project(c, HALF, HALF)
+        for c in range(EARLY_CHUNKS, CHUNKS):
+            project(c, 0, SLOTS)

@@ -19,15 +19,20 @@ EPS = 1e-5
 PACK = 4
 K_PASS = P * PACK
 PASSES = DIM // K_PASS
-SLOTS = BATCH * SEQ // P
-HALF = SLOTS // 2
+HALVES = 2
+PAIR = BATCH // HALVES
+HALF = PAIR * SEQ // P
+SLOTS = HALVES * HALF
 CHUNK = 512
 CHUNK_HEADS = CHUNK // HEAD_DIM
 CHUNKS = 3 * HEADS * HEAD_DIM // CHUNK
 ROW_BLOCKS = CHUNK // P
 BN_WIDTH = 512
 
-EARLY_CHUNKS = HALF
+EARLY = 3
+LATE_SORTS = {4: (3,), 6: (4,), 8: (5,)}
+LATE_FLIPS = {5: (3,), 8: (4,)}
+VECTOR_PARITY = 1
 
 FLOPS = 2 * BATCH * SEQ * DIM * 3 * HEADS * HEAD_DIM
 
@@ -39,213 +44,264 @@ def tile_traceableencoderlayer_pa_kernel(tc, x, ln1_w, qkv_w, out_0, out_1, out_
     with ExitStack() as ctx:
         keep = ctx.enter_context(tc.tile_pool(name="keep", bufs=1))
         small = ctx.enter_context(tc.tile_pool(name="small", bufs=4))
-        stage = ctx.enter_context(tc.tile_pool(name="stage", bufs=2))
+        stage = ctx.enter_context(tc.tile_pool(name="stage", bufs=3))
         w_pool = ctx.enter_context(tc.tile_pool(name="w_pool", bufs=CHUNKS))
-        res_pool = ctx.enter_context(tc.tile_pool(name="res_pool", bufs=4))
+        res_pool = ctx.enter_context(tc.tile_pool(name="res_pool", bufs=5))
         psum = ctx.enter_context(tc.psum_pool(name="psum", bufs=8))
         ctx.enter_context(tc.manual_schedule())
 
-        x_sb = keep.tile([P, SLOTS, DIM], BF16)
+        gain_row = keep.tile([P, DIM], BF16)
+        nc.vector.memset(gain_row[:].bitcast(F32), 0.0)
+
+        x_rows = {}
         w_rows = qkv_w.rearrange("(c a p) k -> c p a k", a=ROW_BLOCKS, p=P)
-        w_raw = []
+        w_raw = {}
 
         def load_tokens(first_slot, n_slots):
-            slots = slice(first_slot, first_slot + n_slots)
-            for b in range(BATCH):
+            half, r = divmod(first_slot, HALF)
+            x_sb = keep.tile([P, n_slots, DIM], BF16, name="x_sb%d" % first_slot)
+            for j in range(n_slots):
+                x_rows[first_slot + j] = x_sb[:, j, :]
+            for b in range(PAIR):
                 nc.sync.dma_start(
-                    out=x_sb[b:P:BATCH, slots, :],
-                    in_=x[b].rearrange("(i r) k -> i r k", r=SLOTS)[:, slots, :],
+                    out=x_sb[b:P:PAIR],
+                    in_=x[PAIR * half + b].rearrange("(i r) k -> i r k", r=HALF)[:, r : r + n_slots, :],
                 )
 
         def load_weights(c):
             raw = w_pool.tile([P, ROW_BLOCKS, DIM], BF16, name="raw")
             nc.sync.dma_start(out=raw[:], in_=w_rows[c])
-            w_raw.append(raw)
+            w_raw[c] = raw
 
-        load_tokens(0, 2)
-        load_tokens(2, 2)
+        load_tokens(0, 1)
+        nc.sync.dma_start(out=gain_row[0:1, :], in_=ln1_w.unsqueeze(0))
+        load_tokens(1, 1)
         load_weights(0)
+        load_tokens(2, 2)
+        load_weights(1)
         load_tokens(4, 2)
+        load_weights(2)
         load_tokens(6, 2)
-        for c in range(1, CHUNKS):
+        for c in range(3, CHUNKS):
             load_weights(c)
 
+        ones = keep.tile([P, P], BF16)
+        nc.vector.memset(ones[:], 1.0)
+        table_warmer = keep.tile([P, 1], F32)
+        nc.scalar.activation(out=table_warmer[:], in_=ones[:, 0:1], func=ACT.Abs_reciprocal_sqrt)
         identity = keep.tile([P, P], F32)
         make_identity(nc, identity[:])
-        minus_half = keep.tile([P, 2], F32)
-        nc.gpsimd.memset(minus_half[:], -0.5)
-        table_warmer = keep.tile([P, 1], F32)
-        nc.scalar.activation(out=table_warmer[:], in_=minus_half[:, 0:1], func=ACT.Identity)
 
-        gain_rows = keep.tile([P, K_PASS], BF16)
-        nc.vector.memset(gain_rows[:], 0.0)
-        nc.scalar.dma_start(
-            out=gain_rows[0:PASSES, :], in_=ln1_w.rearrange("(r c) -> r c", c=K_PASS)
-        )
-        gain_flip = psum.tile([P, PACK, P], F32, tag="bank")
-        for u in range(2):
-            nc.tensor.transpose(
-                gain_flip[:, u, :], gain_rows[:].bitcast(F32)[:, u : 2 * P : 2], identity[:]
+        gain = keep.tile([P, 2, DIM // PACK, 2], BF16)
+        for g in range(PASSES):
+            spread = psum.tile([P, K_PASS], F32, tag="bank")
+            nc.tensor.matmul(
+                spread[:], lhsT=ones[:], rhs=gain_row[:, g * K_PASS : (g + 1) * K_PASS], start=True, stop=True
             )
-        gain_words = keep.tile([P, PASSES, 2], F32)
-        gain = keep.tile([P, PASSES, PACK], F32)
-
-        def widen_gain():
-            nc.vector.tensor_copy(
-                out=gain_words[:], in_=gain_flip[:, 0:2, 0:PASSES].rearrange("p u g -> p g u")
-            )
-            nc.vector.tensor_copy(
-                out=gain[:].rearrange("p g j -> p (g j)"),
-                in_=gain_words[:].rearrange("p g u -> p (g u)").bitcast(BF16),
+            nc.scalar.copy(
+                out=gain[:, :, g * P : (g + 1) * P, :],
+                in_=spread[:].rearrange("p (w u e) -> p u w e", u=2, e=2),
             )
 
         mean_var = keep.tile([P, SLOTS, 2], F32)
-        neg_mean = keep.tile([P, SLOTS], F32)
-        var_eps = keep.tile([P, SLOTS], F32)
         rstd = keep.tile([P, SLOTS], F32)
         shift = keep.tile([P, SLOTS], F32)
         h_codes = keep.tile([P, SLOTS, PASSES, P], U32, align_bytes=64)
         h_scales = keep.tile([P, SLOTS, PASSES, P], U8, align_bytes=64)
         w_codes = keep.tile([P, CHUNKS, PASSES, CHUNK], U32, align_bytes=64)
         w_scales = keep.tile([P, CHUNKS, PASSES, CHUNK], U8, align_bytes=64)
-        z_tiles = {}
-        h_grouped_tiles = {}
-        w_grouped_tiles = {}
+        h_rows = {}
+        h_flips = {}
+        h_grouped = {}
+        w_sorted = {}
+        w_flips = {}
+        w_grouped = {}
+        products = {}
+        results = {}
 
-        def statistics(first_slot):
-            pair = slice(first_slot, first_slot + 2)
-            for r in range(first_slot, first_slot + 2):
-                stats = small.tile([P, DIM // BN_WIDTH, 6], F32)
-                for s in range(DIM // BN_WIDTH):
-                    nc.vector.bn_stats(
-                        out=stats[:, s, :], in_=x_sb[:, r, s * BN_WIDTH : (s + 1) * BN_WIDTH]
-                    )
-                nc.vector.bn_aggr(out=mean_var[:, r, :], in_=stats[:].rearrange("p s f -> p (s f)"))
-            nc.vector.tensor_scalar_mul(out=neg_mean[:, pair], in0=mean_var[:, pair, 0], scalar1=-1.0)
-            nc.gpsimd.tensor_scalar_add(out=var_eps[:, pair], in0=mean_var[:, pair, 1], scalar1=EPS)
-            nc.gpsimd.tensor_tensor(
-                out=rstd[:, pair], in0=var_eps[:, pair], in1=minus_half[:], op=ALU.pow
+        def statistics(r):
+            stats = small.tile([P, DIM // BN_WIDTH, 6], F32)
+            for s in range(DIM // BN_WIDTH):
+                nc.vector.bn_stats(out=stats[:, s, :], in_=x_rows[r][:, s * BN_WIDTH : (s + 1) * BN_WIDTH])
+            nc.vector.bn_aggr(out=mean_var[:, r, :], in_=stats[:].rearrange("p s f -> p (s f)"))
+
+        def scale_rows(r):
+            nc.scalar.activation(
+                out=rstd[:, r : r + 1], in_=mean_var[:, r, 1:2], func=ACT.Abs_reciprocal_sqrt, bias=EPS
             )
-            nc.gpsimd.tensor_tensor(
-                out=shift[:, pair], in0=neg_mean[:, pair], in1=rstd[:, pair], op=ALU.mult
+
+        def shift_rows(r):
+            nc.vector.tensor_scalar(
+                out=shift[:, r : r + 1],
+                in0=mean_var[:, r, 0:1],
+                scalar1=rstd[:, r : r + 1],
+                scalar2=-1.0,
+                op0=ALU.mult,
+                op1=ALU.mult,
             )
 
         def normalise(r):
-            z = stage.tile([P, PASSES, PACK, P], F32, name="z", bufs=4)
+            z = stage.tile([P, 2, DIM // PACK, 2], F32, name="z")
             nc.scalar.activation(
                 out=z[:],
-                in_=x_sb[:, r, :].rearrange("p (g w j) -> p g j w", w=P, j=PACK),
+                in_=x_rows[r].rearrange("p (q u e) -> p u q e", u=2, e=2),
                 func=ACT.Identity,
                 scale=rstd[:, r : r + 1],
                 bias=shift[:, r : r + 1],
             )
-            z_tiles[r] = z
+            h = stage.tile([P, 2, DIM // PACK, 2], BF16, name="h")
+            for u in range(2):
+                nc.gpsimd.tensor_tensor(out=h[:, u], in0=z[:, u], in1=gain[:, u], op=ALU.mult)
+            h_rows[r] = h
 
         def flip_tokens(r):
-            z = z_tiles[r]
-            h_grouped = stage.tile([P, PASSES, P, PACK], BF16, name="h_grouped", align_bytes=64)
+            words = h_rows[r][:].rearrange("p u q e -> p (u q e)").bitcast(F32)
+            flip = psum.tile([P, PASSES, 2, P], F32, tag="bank")
             for g in range(PASSES):
-                z_flip = psum.tile([P, PACK, P], F32, tag="bank")
-                for j in range(PACK):
-                    nc.tensor.transpose(z_flip[:, j, :], z[:, g, j, :], identity[:])
-                nc.vector.tensor_tensor(
-                    out=h_grouped[:, g, :, :],
-                    in0=z_flip[:].rearrange("p j i -> p i j"),
-                    in1=gain[:, g, :].unsqueeze(1).to_broadcast([P, P, PACK]),
-                    op=ALU.mult,
-                )
-            h_grouped_tiles[r] = h_grouped
+                for u in range(2):
+                    first = (u * PASSES + g) * P
+                    nc.tensor.transpose(flip[:, g, u, :], words[:, first : first + P], identity[:])
+            h_flips[r] = flip
+
+        def group_tokens(r):
+            grouped = stage.tile([P, PASSES, P, PACK], BF16, name="grouped", align_bytes=64)
+            nc.scalar.copy(out=grouped[:].bitcast(F32), in_=h_flips[r][:].rearrange("p g u i -> p g i u"))
+            h_grouped[r] = grouped
 
         def quantise_tokens(r):
             nc.vector.quantize_mx(
                 out=h_codes[:, r, :, :].rearrange("p g i -> p (g i)").bitcast(FP8X4),
                 scales=h_scales[:, r, :, :].rearrange("p g i -> p (g i)"),
-                in_=h_grouped_tiles[r][:].rearrange("p g i j -> p (g i j)"),
+                in_=h_grouped[r][:].rearrange("p g i j -> p (g i j)"),
             )
+
+        def sort_weights(c):
+            sorted_words = stage.tile([P, ROW_BLOCKS, 2, DIM // PACK], F32, name="sorted_words", bufs=2)
+            nc.vector.tensor_copy(
+                out=sorted_words[:], in_=w_raw[c][:].bitcast(F32).rearrange("p a (q u) -> p a u q", u=2)
+            )
+            w_sorted[c] = sorted_words
 
         def flip_weights(c):
             words = w_raw[c][:].bitcast(F32)
-            w_grouped = stage.tile([P, PASSES, CHUNK, PACK], BF16, name="w_grouped", align_bytes=64)
-            grouped_words = w_grouped[:].bitcast(F32)
             for g in range(PASSES):
                 for pair in range(ROW_BLOCKS // 2):
-                    w_flip = psum.tile([P, 2, 2, P], F32, tag="bank")
+                    flip = psum.tile([P, 2, 2, P], F32, tag="bank")
                     for u in range(2):
                         for a in range(2):
-                            nc.tensor.transpose(
-                                w_flip[:, u, a, :],
-                                words[:, 2 * pair + a, 2 * P * g + u : 2 * P * (g + 1) : 2],
-                                identity[:],
-                            )
-                    nc.scalar.copy(
-                        out=grouped_words[:, g, 2 * pair * P : (2 * pair + 2) * P, :],
-                        in_=w_flip[:].rearrange("p u a n -> p (a n) u"),
-                    )
-            w_grouped_tiles[c] = w_grouped
+                            if c in w_sorted:
+                                source = w_sorted[c][:, 2 * pair + a, u, g * P : (g + 1) * P]
+                            else:
+                                source = words[:, 2 * pair + a, 2 * P * g + u : 2 * P * (g + 1) : 2]
+                            nc.tensor.transpose(flip[:, u, a, :], source, identity[:])
+                    w_flips[c, 2 * g + pair] = flip
+
+        def group_weights(c, vector_banks):
+            grouped = stage.tile([P, PASSES, CHUNK, PACK], BF16, name="w_grouped", align_bytes=64)
+            grouped_words = grouped[:].bitcast(F32)
+            for bank in range(2 * PASSES):
+                g, pair = divmod(bank, 2)
+                copy = nc.vector.tensor_copy if bank in vector_banks else nc.scalar.copy
+                copy(
+                    out=grouped_words[:, g, 2 * pair * P : (2 * pair + 2) * P, :],
+                    in_=w_flips[c, bank][:].rearrange("p u a n -> p (a n) u"),
+                )
+            w_grouped[c] = grouped
 
         def quantise_weights(c):
-            nc.vector.quantize_mx(
-                out=w_codes[:, c, :, :].rearrange("p g n -> p (g n)").bitcast(FP8X4),
-                scales=w_scales[:, c, :, :].rearrange("p g n -> p (g n)"),
-                in_=w_grouped_tiles[c][:].rearrange("p g n j -> p (g n j)"),
-            )
-
-        def project(c, first_slot, n_slots):
-            result = res_pool.tile([P, CHUNK_HEADS, n_slots, HEAD_DIM], F32, tag="result")
-            for r in range(first_slot, first_slot + n_slots):
-                acc = psum.tile([P, CHUNK], F32, tag="bank")
-                for g in range(PASSES):
-                    nc.tensor.matmul_mx(
-                        out=acc[:],
-                        lhsT=h_codes[:, r, g, :].bitcast(FP8X4),
-                        lhsT_scale=h_scales[:, r, g, :],
-                        rhs=w_codes[:, c, g, :].bitcast(FP8X4),
-                        rhs_scale=w_scales[:, c, g, :],
-                        start=(g == 0),
-                        stop=(g == PASSES - 1),
-                    )
-                by_head = acc[:].rearrange("p (n d) -> p n d", d=HEAD_DIM)
-                if r % 2 == 0:
-                    nc.scalar.copy(out=result[:, :, r - first_slot, :], in_=by_head)
-                else:
-                    nc.vector.tensor_copy(out=result[:, :, r - first_slot, :], in_=by_head)
-            which, first_head = divmod(c * CHUNK_HEADS, HEADS)
-            for b in range(BATCH):
-                nc.sync.dma_start(
-                    out=outs[which][b, first_head : first_head + CHUNK_HEADS].rearrange(
-                        "n (i r) d -> i n r d", r=SLOTS
-                    )[:, :, first_slot : first_slot + n_slots, :],
-                    in_=result[b:P:BATCH],
+            for g in range(PASSES):
+                nc.vector.quantize_mx(
+                    out=w_codes[:, c, g, :].bitcast(FP8X4),
+                    scales=w_scales[:, c, g, :],
+                    in_=w_grouped[c][:, g, :, :].rearrange("p n j -> p (n j)"),
                 )
 
-        for first_slot in range(0, SLOTS, 2):
-            statistics(first_slot)
-        widen_gain()
-        flip_weights(0)
-        for r in range(HALF):
-            normalise(r)
-        flip_tokens(0)
-        flip_tokens(1)
-        quantise_tokens(0)
-        quantise_weights(0)
-        for r in range(2, HALF):
-            flip_tokens(r)
-            quantise_tokens(r - 1)
-        quantise_tokens(HALF - 1)
-        flip_weights(1)
-        normalise(HALF)
-        quantise_weights(1)
+        def multiply(c, r):
+            acc = psum.tile([P, CHUNK], F32, tag="bank")
+            for g in range(PASSES):
+                nc.tensor.matmul_mx(
+                    out=acc[:],
+                    lhsT=h_codes[:, r, g, :].bitcast(FP8X4),
+                    lhsT_scale=h_scales[:, r, g, :],
+                    rhs=w_codes[:, c, g, :].bitcast(FP8X4),
+                    rhs_scale=w_scales[:, c, g, :],
+                    start=(g == 0),
+                    stop=(g == PASSES - 1),
+                )
+            products[c, r] = acc
 
-        for i in range(HALF):
-            flip_weights(i + 2)
-            project(i, 0, HALF)
-            if HALF + i + 1 < SLOTS:
-                normalise(HALF + i + 1)
-            flip_tokens(HALF + i)
-            quantise_tokens(HALF + i)
-            quantise_weights(i + 2)
+        def take_out(c, r):
+            half, slot = divmod(r, HALF)
+            if slot == 0:
+                result = res_pool.tile([P, CHUNK_HEADS, HALF, HEAD_DIM], F32, name="result")
+                results[c, half] = [result, 0]
+            result, taken = results[c, half]
+            copy = nc.vector.tensor_copy if r % 2 == VECTOR_PARITY else nc.scalar.copy
+            copy(out=result[:, :, slot, :], in_=products[c, r][:].rearrange("p (n d) -> p n d", d=HEAD_DIM))
+            results[c, half][1] = taken + 1
+            if taken + 1 == HALF:
+                which, first_head = divmod(c * CHUNK_HEADS, HEADS)
+                for b in range(PAIR):
+                    nc.sync.dma_start(
+                        out=outs[which][PAIR * half + b, first_head : first_head + CHUNK_HEADS].rearrange(
+                            "n (i r) d -> i n r d", r=HALF
+                        ),
+                        in_=result[b:P:PAIR],
+                    )
 
-        for c in range(EARLY_CHUNKS):
-            project(c, HALF, HALF)
-        for c in range(EARLY_CHUNKS, CHUNKS):
-            project(c, 0, SLOTS)
+        statistics(0)
+        scale_rows(0)
+        statistics(1)
+        scale_rows(1)
+        shift_rows(0)
+        normalise(0)
+        shift_rows(1)
+        normalise(1)
+        statistics(2)
+
+        for i in range(SLOTS + 1):
+            ready = [(c, r) for c in range(EARLY) for r in range(SLOTS) if max(c, r) == i - 1]
+            if i < EARLY:
+                flip_weights(i)
+            if i < SLOTS:
+                flip_tokens(i)
+            for c, r in ready:
+                multiply(c, r)
+            for c in LATE_FLIPS.get(i, ()):
+                flip_weights(c)
+            if i + 2 < SLOTS:
+                scale_rows(i + 2)
+            if i < EARLY:
+                group_weights(i, (2,))
+            if i + 2 < SLOTS:
+                shift_rows(i + 2)
+            if i + 3 < SLOTS:
+                statistics(i + 3)
+            if i < SLOTS:
+                group_tokens(i)
+                quantise_tokens(i)
+            if i + 2 < SLOTS:
+                normalise(i + 2)
+            if i < EARLY:
+                quantise_weights(i)
+            for c in LATE_SORTS.get(i, ()):
+                sort_weights(c)
+            for c, r in ready:
+                take_out(c, r)
+            for c in LATE_FLIPS.get(i, ()):
+                group_weights(c, (1, 3))
+                quantise_weights(c)
+
+        for c in range(EARLY, CHUNKS):
+            ahead = c + 1
+            if ahead == CHUNKS - 1:
+                flip_weights(ahead)
+            for r in range(SLOTS):
+                multiply(c, r)
+            for r in range(HALF):
+                take_out(c, r)
+            if ahead == CHUNKS - 1:
+                group_weights(ahead, (1, 3))
+                quantise_weights(ahead)
+            for r in range(HALF, SLOTS):
+                take_out(c, r)

@@ -27,12 +27,25 @@ CHUNK = 512
 CHUNK_HEADS = CHUNK // HEAD_DIM
 CHUNKS = 3 * HEADS * HEAD_DIM // CHUNK
 ROW_BLOCKS = CHUNK // P
+BANKS = 2 * PASSES
 BN_WIDTH = 512
 
-EARLY = 3
-LATE_SORTS = {4: (3,), 6: (4,), 8: (5,)}
-LATE_FLIPS = {5: (3,), 8: (4,)}
-VECTOR_PARITY = 1
+ROUNDS = (
+    ((0,), (0,)),
+    ((1,), (1,)),
+    ((), (2, 3)),
+    ((), (4, 5)),
+    ((), (6, 7)),
+    ((2,), ()),
+    ((3,), ()),
+    ((4,), ()),
+    ((5,), ()),
+    ((), ()),
+)
+LATE = 2
+SORT_AHEAD = 2
+STATS_AHEAD = 3
+NORM_AHEAD = 2
 
 FLOPS = 2 * BATCH * SEQ * DIM * 3 * HEADS * HEAD_DIM
 
@@ -50,8 +63,8 @@ def tile_traceableencoderlayer_pa_kernel(tc, x, ln1_w, qkv_w, out_0, out_1, out_
         psum = ctx.enter_context(tc.psum_pool(name="psum", bufs=8))
         ctx.enter_context(tc.manual_schedule())
 
-        gain_row = keep.tile([P, DIM], BF16)
-        nc.vector.memset(gain_row[:].bitcast(F32), 0.0)
+        gain_rows = keep.tile([P, K_PASS], BF16)
+        nc.vector.memset(gain_rows[:].bitcast(F32), 0.0)
 
         x_rows = {}
         w_rows = qkv_w.rearrange("(c a p) k -> c p a k", a=ROW_BLOCKS, p=P)
@@ -74,34 +87,33 @@ def tile_traceableencoderlayer_pa_kernel(tc, x, ln1_w, qkv_w, out_0, out_1, out_
             w_raw[c] = raw
 
         load_tokens(0, 1)
-        nc.sync.dma_start(out=gain_row[0:1, :], in_=ln1_w.unsqueeze(0))
+        nc.sync.dma_start(out=gain_rows[0:PASSES, :], in_=ln1_w.rearrange("(r c) -> r c", c=K_PASS))
         load_tokens(1, 1)
-        load_weights(0)
         load_tokens(2, 2)
+        load_weights(0)
         load_weights(1)
         load_tokens(4, 2)
-        load_weights(2)
         load_tokens(6, 2)
-        for c in range(3, CHUNKS):
+        for c in range(LATE, CHUNKS):
             load_weights(c)
 
-        ones = keep.tile([P, P], BF16)
-        nc.vector.memset(ones[:], 1.0)
+        one = keep.tile([P, 1], F32)
+        nc.vector.memset(one[:], 1.0)
         table_warmer = keep.tile([P, 1], F32)
-        nc.scalar.activation(out=table_warmer[:], in_=ones[:, 0:1], func=ACT.Abs_reciprocal_sqrt)
+        nc.scalar.activation(out=table_warmer[:], in_=one[:], func=ACT.Abs_reciprocal_sqrt)
         identity = keep.tile([P, P], F32)
         make_identity(nc, identity[:])
 
-        gain = keep.tile([P, 2, DIM // PACK, 2], BF16)
-        for g in range(PASSES):
-            spread = psum.tile([P, K_PASS], F32, tag="bank")
-            nc.tensor.matmul(
-                spread[:], lhsT=ones[:], rhs=gain_row[:, g * K_PASS : (g + 1) * K_PASS], start=True, stop=True
-            )
-            nc.scalar.copy(
-                out=gain[:, :, g * P : (g + 1) * P, :],
-                in_=spread[:].rearrange("p (w u e) -> p u w e", u=2, e=2),
-            )
+        gain_flip = psum.tile([P, PACK, P], F32, tag="bank")
+        for u in range(2):
+            nc.tensor.transpose(gain_flip[:, u, :], gain_rows[:].bitcast(F32)[:, u : 2 * P : 2], identity[:])
+        gain_words = keep.tile([P, PASSES, 2], F32)
+        nc.scalar.copy(out=gain_words[:], in_=gain_flip[:, 0:2, 0:PASSES].rearrange("p u g -> p g u"))
+        gain = keep.tile([P, PASSES, PACK], F32)
+        nc.scalar.copy(
+            out=gain[:].rearrange("p g j -> p (g j)"),
+            in_=gain_words[:].rearrange("p g u -> p (g u)").bitcast(BF16),
+        )
 
         mean_var = keep.tile([P, SLOTS, 2], F32)
         rstd = keep.tile([P, SLOTS], F32)
@@ -110,8 +122,8 @@ def tile_traceableencoderlayer_pa_kernel(tc, x, ln1_w, qkv_w, out_0, out_1, out_
         h_scales = keep.tile([P, SLOTS, PASSES, P], U8, align_bytes=64)
         w_codes = keep.tile([P, CHUNKS, PASSES, CHUNK], U32, align_bytes=64)
         w_scales = keep.tile([P, CHUNKS, PASSES, CHUNK], U8, align_bytes=64)
-        h_rows = {}
-        h_flips = {}
+        z_tiles = {}
+        z_flips = {}
         h_grouped = {}
         w_sorted = {}
         w_flips = {}
@@ -124,8 +136,6 @@ def tile_traceableencoderlayer_pa_kernel(tc, x, ln1_w, qkv_w, out_0, out_1, out_
             for s in range(DIM // BN_WIDTH):
                 nc.vector.bn_stats(out=stats[:, s, :], in_=x_rows[r][:, s * BN_WIDTH : (s + 1) * BN_WIDTH])
             nc.vector.bn_aggr(out=mean_var[:, r, :], in_=stats[:].rearrange("p s f -> p (s f)"))
-
-        def scale_rows(r):
             nc.scalar.activation(
                 out=rstd[:, r : r + 1], in_=mean_var[:, r, 1:2], func=ACT.Abs_reciprocal_sqrt, bias=EPS
             )
@@ -141,31 +151,33 @@ def tile_traceableencoderlayer_pa_kernel(tc, x, ln1_w, qkv_w, out_0, out_1, out_
             )
 
         def normalise(r):
-            z = stage.tile([P, 2, DIM // PACK, 2], F32, name="z")
-            nc.scalar.activation(
+            z = stage.tile([P, PASSES, PACK, P], F32, name="z")
+            nc.gpsimd.tensor_scalar(
                 out=z[:],
-                in_=x_rows[r].rearrange("p (q u e) -> p u q e", u=2, e=2),
-                func=ACT.Identity,
-                scale=rstd[:, r : r + 1],
-                bias=shift[:, r : r + 1],
+                in0=x_rows[r].rearrange("p (g w j) -> p g j w", w=P, j=PACK),
+                scalar1=rstd[:, r : r + 1],
+                scalar2=shift[:, r : r + 1],
+                op0=ALU.mult,
+                op1=ALU.add,
             )
-            h = stage.tile([P, 2, DIM // PACK, 2], BF16, name="h")
-            for u in range(2):
-                nc.gpsimd.tensor_tensor(out=h[:, u], in0=z[:, u], in1=gain[:, u], op=ALU.mult)
-            h_rows[r] = h
+            z_tiles[r] = z
 
         def flip_tokens(r):
-            words = h_rows[r][:].rearrange("p u q e -> p (u q e)").bitcast(F32)
-            flip = psum.tile([P, PASSES, 2, P], F32, tag="bank")
             for g in range(PASSES):
-                for u in range(2):
-                    first = (u * PASSES + g) * P
-                    nc.tensor.transpose(flip[:, g, u, :], words[:, first : first + P], identity[:])
-            h_flips[r] = flip
+                flip = psum.tile([P, PACK, P], F32, tag="bank")
+                for j in range(PACK):
+                    nc.tensor.transpose(flip[:, j, :], z_tiles[r][:, g, j, :], identity[:])
+                z_flips[r, g] = flip
 
         def group_tokens(r):
             grouped = stage.tile([P, PASSES, P, PACK], BF16, name="grouped", align_bytes=64)
-            nc.scalar.copy(out=grouped[:].bitcast(F32), in_=h_flips[r][:].rearrange("p g u i -> p g i u"))
+            for g in range(PASSES):
+                nc.vector.tensor_tensor(
+                    out=grouped[:, g, :, :],
+                    in0=z_flips[r, g][:].rearrange("p j i -> p i j"),
+                    in1=gain[:, g, :].unsqueeze(1).to_broadcast([P, P, PACK]),
+                    op=ALU.mult,
+                )
             h_grouped[r] = grouped
 
         def quantise_tokens(r):
@@ -176,7 +188,7 @@ def tile_traceableencoderlayer_pa_kernel(tc, x, ln1_w, qkv_w, out_0, out_1, out_
             )
 
         def sort_weights(c):
-            sorted_words = stage.tile([P, ROW_BLOCKS, 2, DIM // PACK], F32, name="sorted_words", bufs=2)
+            sorted_words = stage.tile([P, ROW_BLOCKS, 2, DIM // PACK], F32, name="sorted_words")
             nc.vector.tensor_copy(
                 out=sorted_words[:], in_=w_raw[c][:].bitcast(F32).rearrange("p a (q u) -> p a u q", u=2)
             )
@@ -199,7 +211,7 @@ def tile_traceableencoderlayer_pa_kernel(tc, x, ln1_w, qkv_w, out_0, out_1, out_
         def group_weights(c, vector_banks):
             grouped = stage.tile([P, PASSES, CHUNK, PACK], BF16, name="w_grouped", align_bytes=64)
             grouped_words = grouped[:].bitcast(F32)
-            for bank in range(2 * PASSES):
+            for bank in range(BANKS):
                 g, pair = divmod(bank, 2)
                 copy = nc.vector.tensor_copy if bank in vector_banks else nc.scalar.copy
                 copy(
@@ -230,16 +242,14 @@ def tile_traceableencoderlayer_pa_kernel(tc, x, ln1_w, qkv_w, out_0, out_1, out_
                 )
             products[c, r] = acc
 
-        def take_out(c, r):
+        def take_out(c, r, copy):
             half, slot = divmod(r, HALF)
             if slot == 0:
                 result = res_pool.tile([P, CHUNK_HEADS, HALF, HEAD_DIM], F32, name="result")
-                results[c, half] = [result, 0]
-            result, taken = results[c, half]
-            copy = nc.vector.tensor_copy if r % 2 == VECTOR_PARITY else nc.scalar.copy
+                results[c, half] = result
+            result = results[c, half]
             copy(out=result[:, :, slot, :], in_=products[c, r][:].rearrange("p (n d) -> p n d", d=HEAD_DIM))
-            results[c, half][1] = taken + 1
-            if taken + 1 == HALF:
+            if slot == HALF - 1:
                 which, first_head = divmod(c * CHUNK_HEADS, HEADS)
                 for b in range(PAIR):
                     nc.sync.dma_start(
@@ -249,59 +259,48 @@ def tile_traceableencoderlayer_pa_kernel(tc, x, ln1_w, qkv_w, out_0, out_1, out_
                         in_=result[b:P:PAIR],
                     )
 
-        statistics(0)
-        scale_rows(0)
-        statistics(1)
-        scale_rows(1)
-        shift_rows(0)
-        normalise(0)
-        shift_rows(1)
-        normalise(1)
-        statistics(2)
+        for r in range(STATS_AHEAD):
+            statistics(r)
+            if r > 0:
+                shift_rows(r - 1)
+        for r in range(NORM_AHEAD):
+            normalise(r)
 
-        for i in range(SLOTS + 1):
-            ready = [(c, r) for c in range(EARLY) for r in range(SLOTS) if max(c, r) == i - 1]
-            if i < EARLY:
-                flip_weights(i)
-            if i < SLOTS:
-                flip_tokens(i)
-            for c, r in ready:
-                multiply(c, r)
-            for c in LATE_FLIPS.get(i, ()):
+        ready_chunks = []
+        ready_slots = []
+        done = set()
+        for i in range(len(ROUNDS)):
+            chunks, slots = ROUNDS[i]
+            units = [(c, r) for c in ready_chunks for r in ready_slots if (c, r) not in done]
+            for r in slots:
+                flip_tokens(r)
+            for c in chunks:
                 flip_weights(c)
-            if i + 2 < SLOTS:
-                scale_rows(i + 2)
-            if i < EARLY:
-                group_weights(i, (2,))
-            if i + 2 < SLOTS:
-                shift_rows(i + 2)
-            if i + 3 < SLOTS:
-                statistics(i + 3)
-            if i < SLOTS:
-                group_tokens(i)
-                quantise_tokens(i)
-            if i + 2 < SLOTS:
-                normalise(i + 2)
-            if i < EARLY:
-                quantise_weights(i)
-            for c in LATE_SORTS.get(i, ()):
-                sort_weights(c)
-            for c, r in ready:
-                take_out(c, r)
-            for c in LATE_FLIPS.get(i, ()):
-                group_weights(c, (1, 3))
-                quantise_weights(c)
-
-        for c in range(EARLY, CHUNKS):
-            ahead = c + 1
-            if ahead == CHUNKS - 1:
-                flip_weights(ahead)
-            for r in range(SLOTS):
+            for c, r in units:
                 multiply(c, r)
-            for r in range(HALF):
-                take_out(c, r)
-            if ahead == CHUNKS - 1:
-                group_weights(ahead, (1, 3))
-                quantise_weights(ahead)
-            for r in range(HALF, SLOTS):
-                take_out(c, r)
+            for c in chunks:
+                group_weights(c, () if c < LATE else (2,))
+            for r in slots:
+                if r + STATS_AHEAD < SLOTS:
+                    statistics(r + STATS_AHEAD)
+            for r in slots:
+                if r + NORM_AHEAD < SLOTS:
+                    shift_rows(r + NORM_AHEAD)
+                    normalise(r + NORM_AHEAD)
+            for r in slots:
+                group_tokens(r)
+            for r in slots:
+                quantise_tokens(r)
+            for c in chunks:
+                quantise_weights(c)
+            if i + SORT_AHEAD < len(ROUNDS):
+                for c in ROUNDS[i + SORT_AHEAD][0]:
+                    if c >= LATE:
+                        sort_weights(c)
+            for c, r in units:
+                late_third = c >= LATE and (c * SLOTS + r) % 3 == 2
+                take_out(c, r, nc.vector.tensor_copy if late_third else nc.scalar.copy)
+            for u in units:
+                done.add(u)
+            ready_chunks.extend(chunks)
+            ready_slots.extend(slots)

@@ -31,9 +31,8 @@ BANKS = 2 * PASSES
 BN_WIDTH = 512
 
 ROUNDS = (
-    ((0,), (0,)),
-    ((1,), (1,)),
-    ((), (2, 3)),
+    ((0,), (0, 1)),
+    ((1,), (2, 3)),
     ((), (4, 5)),
     ((), (6, 7)),
     ((2,), ()),
@@ -58,7 +57,6 @@ def tile_traceableencoderlayer_pa_kernel(tc, x, ln1_w, qkv_w, out_0, out_1, out_
         keep = ctx.enter_context(tc.tile_pool(name="keep", bufs=1))
         small = ctx.enter_context(tc.tile_pool(name="small", bufs=4))
         stage = ctx.enter_context(tc.tile_pool(name="stage", bufs=3))
-        w_pool = ctx.enter_context(tc.tile_pool(name="w_pool", bufs=CHUNKS))
         res_pool = ctx.enter_context(tc.tile_pool(name="res_pool", bufs=5))
         psum = ctx.enter_context(tc.psum_pool(name="psum", bufs=8))
         ctx.enter_context(tc.manual_schedule())
@@ -69,6 +67,7 @@ def tile_traceableencoderlayer_pa_kernel(tc, x, ln1_w, qkv_w, out_0, out_1, out_
         x_rows = {}
         w_rows = qkv_w.rearrange("(c a p) k -> c p a k", a=ROW_BLOCKS, p=P)
         w_raw = {}
+        w_whole = {}
 
         def load_tokens(first_slot, n_slots):
             half, r = divmod(first_slot, HALF)
@@ -82,17 +81,22 @@ def tile_traceableencoderlayer_pa_kernel(tc, x, ln1_w, qkv_w, out_0, out_1, out_
                 )
 
         def load_weights(c):
-            raw = w_pool.tile([P, ROW_BLOCKS, DIM], BF16, name="raw")
-            nc.sync.dma_start(out=raw[:], in_=w_rows[c])
-            w_raw[c] = raw
+            pieces = 2 if c == 0 else 1
+            blocks = ROW_BLOCKS // pieces
+            for first in range(0, ROW_BLOCKS, blocks):
+                raw = keep.tile([P, blocks, DIM], BF16, name="raw%d_%d" % (c, first))
+                nc.sync.dma_start(out=raw[:], in_=w_rows[c][:, first : first + blocks, :])
+                for a in range(blocks):
+                    w_raw[c, first + a] = raw[:, a, :]
+                w_whole[c] = raw
 
         load_tokens(0, 1)
         nc.sync.dma_start(out=gain_rows[0:PASSES, :], in_=ln1_w.rearrange("(r c) -> r c", c=K_PASS))
         load_tokens(1, 1)
         load_tokens(2, 2)
         load_weights(0)
-        load_weights(1)
         load_tokens(4, 2)
+        load_weights(1)
         load_tokens(6, 2)
         for c in range(LATE, CHUNKS):
             load_weights(c)
@@ -136,12 +140,12 @@ def tile_traceableencoderlayer_pa_kernel(tc, x, ln1_w, qkv_w, out_0, out_1, out_
             for s in range(DIM // BN_WIDTH):
                 nc.vector.bn_stats(out=stats[:, s, :], in_=x_rows[r][:, s * BN_WIDTH : (s + 1) * BN_WIDTH])
             nc.vector.bn_aggr(out=mean_var[:, r, :], in_=stats[:].rearrange("p s f -> p (s f)"))
+
+        def normalise(r):
             nc.scalar.activation(
                 out=rstd[:, r : r + 1], in_=mean_var[:, r, 1:2], func=ACT.Abs_reciprocal_sqrt, bias=EPS
             )
-
-        def shift_rows(r):
-            nc.vector.tensor_scalar(
+            nc.gpsimd.tensor_scalar(
                 out=shift[:, r : r + 1],
                 in0=mean_var[:, r, 0:1],
                 scalar1=rstd[:, r : r + 1],
@@ -149,8 +153,6 @@ def tile_traceableencoderlayer_pa_kernel(tc, x, ln1_w, qkv_w, out_0, out_1, out_
                 op0=ALU.mult,
                 op1=ALU.mult,
             )
-
-        def normalise(r):
             z = stage.tile([P, PASSES, PACK, P], F32, name="z")
             nc.gpsimd.tensor_scalar(
                 out=z[:],
@@ -190,33 +192,36 @@ def tile_traceableencoderlayer_pa_kernel(tc, x, ln1_w, qkv_w, out_0, out_1, out_
         def sort_weights(c):
             sorted_words = stage.tile([P, ROW_BLOCKS, 2, DIM // PACK], F32, name="sorted_words")
             nc.vector.tensor_copy(
-                out=sorted_words[:], in_=w_raw[c][:].bitcast(F32).rearrange("p a (q u) -> p a u q", u=2)
+                out=sorted_words[:], in_=w_whole[c][:].bitcast(F32).rearrange("p a (q u) -> p a u q", u=2)
             )
             w_sorted[c] = sorted_words
 
-        def flip_weights(c):
-            words = w_raw[c][:].bitcast(F32)
-            for g in range(PASSES):
-                for pair in range(ROW_BLOCKS // 2):
-                    flip = psum.tile([P, 2, 2, P], F32, tag="bank")
-                    for u in range(2):
-                        for a in range(2):
-                            if c in w_sorted:
-                                source = w_sorted[c][:, 2 * pair + a, u, g * P : (g + 1) * P]
-                            else:
-                                source = words[:, 2 * pair + a, 2 * P * g + u : 2 * P * (g + 1) : 2]
-                            nc.tensor.transpose(flip[:, u, a, :], source, identity[:])
-                    w_flips[c, 2 * g + pair] = flip
+        def bank_order(c):
+            if c == 0:
+                return [(g, pair) for pair in range(2) for g in range(PASSES)]
+            return [(g, pair) for g in range(PASSES) for pair in range(2)]
 
-        def group_weights(c, vector_banks):
+        def flip_weights(c):
+            for g, pair in bank_order(c):
+                flip = psum.tile([P, 2, 2, P], F32, tag="bank")
+                for u in range(2):
+                    for a in range(2):
+                        block = 2 * pair + a
+                        if c in w_sorted:
+                            source = w_sorted[c][:, block, u, g * P : (g + 1) * P]
+                        else:
+                            source = w_raw[c, block].bitcast(F32)[:, 2 * P * g + u : 2 * P * (g + 1) : 2]
+                        nc.tensor.transpose(flip[:, u, a, :], source, identity[:])
+                w_flips[c, g, pair] = flip
+
+        def group_weights(c):
             grouped = stage.tile([P, PASSES, CHUNK, PACK], BF16, name="w_grouped", align_bytes=64)
             grouped_words = grouped[:].bitcast(F32)
-            for bank in range(BANKS):
-                g, pair = divmod(bank, 2)
-                copy = nc.vector.tensor_copy if bank in vector_banks else nc.scalar.copy
+            for g, pair in bank_order(c):
+                copy = nc.vector.tensor_copy if c >= LATE and pair == 1 else nc.scalar.copy
                 copy(
                     out=grouped_words[:, g, 2 * pair * P : (2 * pair + 2) * P, :],
-                    in_=w_flips[c, bank][:].rearrange("p u a n -> p (a n) u"),
+                    in_=w_flips[c, g, pair][:].rearrange("p u a n -> p (a n) u"),
                 )
             w_grouped[c] = grouped
 
@@ -262,9 +267,7 @@ def tile_traceableencoderlayer_pa_kernel(tc, x, ln1_w, qkv_w, out_0, out_1, out_
         for r in range(STATS_AHEAD):
             statistics(r)
             if r > 0:
-                shift_rows(r - 1)
-        for r in range(NORM_AHEAD):
-            normalise(r)
+                normalise(r - 1)
 
         ready_chunks = []
         ready_slots = []
@@ -272,27 +275,26 @@ def tile_traceableencoderlayer_pa_kernel(tc, x, ln1_w, qkv_w, out_0, out_1, out_
         for i in range(len(ROUNDS)):
             chunks, slots = ROUNDS[i]
             units = [(c, r) for c in ready_chunks for r in ready_slots if (c, r) not in done]
-            for r in slots:
-                flip_tokens(r)
             for c in chunks:
                 flip_weights(c)
+            for r in slots:
+                flip_tokens(r)
             for c, r in units:
                 multiply(c, r)
             for c in chunks:
-                group_weights(c, () if c < LATE else (2,))
+                group_weights(c)
             for r in slots:
                 if r + STATS_AHEAD < SLOTS:
                     statistics(r + STATS_AHEAD)
-            for r in slots:
-                if r + NORM_AHEAD < SLOTS:
-                    shift_rows(r + NORM_AHEAD)
-                    normalise(r + NORM_AHEAD)
             for r in slots:
                 group_tokens(r)
             for r in slots:
                 quantise_tokens(r)
             for c in chunks:
                 quantise_weights(c)
+            for r in slots:
+                if r + NORM_AHEAD < SLOTS:
+                    normalise(r + NORM_AHEAD)
             if i + SORT_AHEAD < len(ROUNDS):
                 for c in ROUNDS[i + SORT_AHEAD][0]:
                     if c >= LATE:

@@ -43,6 +43,8 @@ ROUNDS = (
 )
 LATE = 2
 SORT_AHEAD = 2
+SCALAR_STATS = (5, 7)
+SCALAR_AHEAD = 5
 STATS_AHEAD = 3
 NORM_AHEAD = 2
 
@@ -122,6 +124,9 @@ def tile_traceableencoderlayer_pa_kernel(tc, x, ln1_w, qkv_w, out_0, out_1, out_
         mean_var = keep.tile([P, SLOTS, 2], F32)
         rstd = keep.tile([P, SLOTS], F32)
         shift = keep.tile([P, SLOTS], F32)
+        sums = keep.tile([P, SLOTS], F32)
+        minus_mean = keep.tile([P, SLOTS], F32)
+        squares = keep.tile([P, SLOTS], F32)
         h_codes = keep.tile([P, SLOTS, PASSES, P], U32, align_bytes=64)
         h_scales = keep.tile([P, SLOTS, PASSES, P], U8, align_bytes=64)
         w_codes = keep.tile([P, CHUNKS, PASSES, CHUNK], U32, align_bytes=64)
@@ -136,20 +141,41 @@ def tile_traceableencoderlayer_pa_kernel(tc, x, ln1_w, qkv_w, out_0, out_1, out_
         results = {}
 
         def statistics(r):
+            if r in SCALAR_STATS:
+                unused = stage.tile([P, DIM], BF16, name="unused")
+                nc.scalar.activation(
+                    out=unused[:], in_=x_rows[r], func=ACT.Identity, accum_out=sums[:, r : r + 1]
+                )
+                nc.scalar.activation(
+                    out=minus_mean[:, r : r + 1], in_=sums[:, r : r + 1], func=ACT.Copy, scale=-1.0 / DIM
+                )
+                nc.scalar.activation(
+                    out=unused[:],
+                    in_=x_rows[r],
+                    func=ACT.Square,
+                    bias=minus_mean[:, r : r + 1],
+                    accum_out=squares[:, r : r + 1],
+                )
+                return
             stats = small.tile([P, DIM // BN_WIDTH, 6], F32)
             for s in range(DIM // BN_WIDTH):
                 nc.vector.bn_stats(out=stats[:, s, :], in_=x_rows[r][:, s * BN_WIDTH : (s + 1) * BN_WIDTH])
             nc.vector.bn_aggr(out=mean_var[:, r, :], in_=stats[:].rearrange("p s f -> p (s f)"))
 
         def normalise(r):
+            from_scalar = r in SCALAR_STATS
             nc.scalar.activation(
-                out=rstd[:, r : r + 1], in_=mean_var[:, r, 1:2], func=ACT.Abs_reciprocal_sqrt, bias=EPS
+                out=rstd[:, r : r + 1],
+                in_=squares[:, r : r + 1] if from_scalar else mean_var[:, r, 1:2],
+                func=ACT.Abs_reciprocal_sqrt,
+                scale=1.0 / DIM if from_scalar else 1.0,
+                bias=EPS,
             )
             nc.gpsimd.tensor_scalar(
                 out=shift[:, r : r + 1],
-                in0=mean_var[:, r, 0:1],
+                in0=minus_mean[:, r : r + 1] if from_scalar else mean_var[:, r, 0:1],
                 scalar1=rstd[:, r : r + 1],
-                scalar2=-1.0,
+                scalar2=1.0 if from_scalar else -1.0,
                 op0=ALU.mult,
                 op1=ALU.mult,
             )
@@ -172,21 +198,22 @@ def tile_traceableencoderlayer_pa_kernel(tc, x, ln1_w, qkv_w, out_0, out_1, out_
                 z_flips[r, g] = flip
 
         def group_tokens(r):
-            grouped = stage.tile([P, PASSES, P, PACK], BF16, name="grouped", align_bytes=64)
+            if r % 2 == 0:
+                pair = stage.tile([P, 2, PASSES, P, PACK], BF16, name="pair", align_bytes=64)
+                h_grouped[r] = pair
             for g in range(PASSES):
                 nc.vector.tensor_tensor(
-                    out=grouped[:, g, :, :],
+                    out=h_grouped[r - r % 2][:, r % 2, g, :, :],
                     in0=z_flips[r, g][:].rearrange("p j i -> p i j"),
                     in1=gain[:, g, :].unsqueeze(1).to_broadcast([P, P, PACK]),
                     op=ALU.mult,
                 )
-            h_grouped[r] = grouped
 
         def quantise_tokens(r):
             nc.vector.quantize_mx(
-                out=h_codes[:, r, :, :].rearrange("p g i -> p (g i)").bitcast(FP8X4),
-                scales=h_scales[:, r, :, :].rearrange("p g i -> p (g i)"),
-                in_=h_grouped[r][:].rearrange("p g i j -> p (g i j)"),
+                out=h_codes[:, r : r + 2].rearrange("p s g i -> p (s g i)").bitcast(FP8X4),
+                scales=h_scales[:, r : r + 2].rearrange("p s g i -> p (s g i)"),
+                in_=h_grouped[r][:].rearrange("p s g i j -> p (s g i j)"),
             )
 
         def sort_weights(c):
@@ -269,6 +296,7 @@ def tile_traceableencoderlayer_pa_kernel(tc, x, ln1_w, qkv_w, out_0, out_1, out_
             if r > 0:
                 normalise(r - 1)
 
+        counted = set(range(STATS_AHEAD))
         ready_chunks = []
         ready_slots = []
         done = set()
@@ -283,18 +311,24 @@ def tile_traceableencoderlayer_pa_kernel(tc, x, ln1_w, qkv_w, out_0, out_1, out_
                 multiply(c, r)
             for c in chunks:
                 group_weights(c)
+            to_normalise = [r + NORM_AHEAD for r in slots if r + NORM_AHEAD < SLOTS]
+            for r in to_normalise:
+                if r in counted:
+                    normalise(r)
+            fresh = [r for r in to_normalise if r not in counted]
             for r in slots:
-                if r + STATS_AHEAD < SLOTS:
+                if r + STATS_AHEAD < SLOTS and r + STATS_AHEAD not in SCALAR_STATS:
                     statistics(r + STATS_AHEAD)
+                if r + SCALAR_AHEAD in SCALAR_STATS:
+                    statistics(r + SCALAR_AHEAD)
             for r in slots:
                 group_tokens(r)
-            for r in slots:
+            for r in slots[::2]:
                 quantise_tokens(r)
             for c in chunks:
                 quantise_weights(c)
-            for r in slots:
-                if r + NORM_AHEAD < SLOTS:
-                    normalise(r + NORM_AHEAD)
+            for r in fresh:
+                normalise(r)
             if i + SORT_AHEAD < len(ROUNDS):
                 for c in ROUNDS[i + SORT_AHEAD][0]:
                     if c >= LATE:
@@ -302,6 +336,9 @@ def tile_traceableencoderlayer_pa_kernel(tc, x, ln1_w, qkv_w, out_0, out_1, out_
             for c, r in units:
                 late_third = c >= LATE and (c * SLOTS + r) % 3 == 2
                 take_out(c, r, nc.vector.tensor_copy if late_third else nc.scalar.copy)
+            for r in slots:
+                counted.add(r + STATS_AHEAD)
+                counted.add(r + SCALAR_AHEAD)
             for u in units:
                 done.add(u)
             ready_chunks.extend(chunks)

@@ -42,6 +42,7 @@ ROUNDS = (
     ((), ()),
 )
 LATE = 2
+STORE_LAG = 1
 SORT_AHEAD = 2
 SCALAR_STATS = (5, 7)
 SCALAR_AHEAD = 5
@@ -138,6 +139,7 @@ def tile_traceableencoderlayer_pa_kernel(tc, x, ln1_w, qkv_w, out_0, out_1, out_
         w_flips = {}
         w_grouped = {}
         products = {}
+        waiting = []
         results = {}
 
         def statistics(r):
@@ -218,7 +220,8 @@ def tile_traceableencoderlayer_pa_kernel(tc, x, ln1_w, qkv_w, out_0, out_1, out_
 
         def sort_weights(c):
             sorted_words = stage.tile([P, ROW_BLOCKS, 2, DIM // PACK], F32, name="sorted_words")
-            nc.vector.tensor_copy(
+            copy = nc.scalar.copy if c == LATE else nc.vector.tensor_copy
+            copy(
                 out=sorted_words[:], in_=w_whole[c][:].bitcast(F32).rearrange("p a (q u) -> p a u q", u=2)
             )
             w_sorted[c] = sorted_words
@@ -282,14 +285,22 @@ def tile_traceableencoderlayer_pa_kernel(tc, x, ln1_w, qkv_w, out_0, out_1, out_
             result = results[c, half]
             copy(out=result[:, :, slot, :], in_=products[c, r][:].rearrange("p (n d) -> p n d", d=HEAD_DIM))
             if slot == HALF - 1:
-                which, first_head = divmod(c * CHUNK_HEADS, HEADS)
-                for b in range(PAIR):
-                    nc.sync.dma_start(
-                        out=outs[which][PAIR * half + b, first_head : first_head + CHUNK_HEADS].rearrange(
-                            "n (i r) d -> i n r d", r=HALF
-                        ),
-                        in_=result[b:P:PAIR],
-                    )
+                store(c, half, 0, nc.sync)
+                if c < LATE:
+                    store(c, half, 1, nc.sync)
+                else:
+                    waiting.append((c, half))
+            if waiting and slot == STORE_LAG:
+                store(*waiting.pop(0), 1, nc.scalar)
+
+        def store(c, half, b, queue):
+            which, first_head = divmod(c * CHUNK_HEADS, HEADS)
+            queue.dma_start(
+                out=outs[which][PAIR * half + b, first_head : first_head + CHUNK_HEADS].rearrange(
+                    "n (i r) d -> i n r d", r=HALF
+                ),
+                in_=results[c, half][b:P:PAIR],
+            )
 
         for r in range(STATS_AHEAD):
             statistics(r)
@@ -339,6 +350,9 @@ def tile_traceableencoderlayer_pa_kernel(tc, x, ln1_w, qkv_w, out_0, out_1, out_
             for r in slots:
                 counted.add(r + STATS_AHEAD)
                 counted.add(r + SCALAR_AHEAD)
+            if i == len(ROUNDS) - 1:
+                for c, half in waiting:
+                    store(c, half, 1, nc.scalar)
             for u in units:
                 done.add(u)
             ready_chunks.extend(chunks)

@@ -31,21 +31,22 @@ BANKS = 2 * PASSES
 BN_WIDTH = 512
 
 ROUNDS = (
-    ((0,), (0, 1)),
-    ((1,), (2, 3)),
-    ((), (4, 5)),
-    ((), (6, 7)),
-    ((2,), ()),
-    ((3,), ()),
-    ((4,), ()),
-    ((5,), ()),
-    ((), ()),
+    ((0,), (0, 1), 0, 0),
+    ((1,), (2, 3), 0, 0),
+    ((), (4, 5), 0, 0),
+    ((), (6, 7), 0, 2),
+    ((2,), (), 0, 0),
+    ((3,), (), 4, 0),
+    ((4,), (), 4, 0),
+    ((5,), (), 4, 0),
+    ((), (), 0, 0),
 )
 LATE = 2
 STORE_LAG = 1
 SORT_AHEAD = 2
 SCALAR_STATS = (5, 7)
 SCALAR_AHEAD = 5
+VECTOR_NORM = (3, 5, 7)
 STATS_AHEAD = 3
 NORM_AHEAD = 2
 
@@ -99,8 +100,8 @@ def tile_traceableencoderlayer_pa_kernel(tc, x, ln1_w, qkv_w, out_0, out_1, out_
         load_tokens(2, 2)
         load_weights(0)
         load_tokens(4, 2)
-        load_weights(1)
         load_tokens(6, 2)
+        load_weights(1)
         for c in range(LATE, CHUNKS):
             load_weights(c)
 
@@ -141,6 +142,7 @@ def tile_traceableencoderlayer_pa_kernel(tc, x, ln1_w, qkv_w, out_0, out_1, out_
         products = {}
         waiting = []
         results = {}
+        uncombined = []
 
         def statistics(r):
             if r in SCALAR_STATS:
@@ -162,7 +164,13 @@ def tile_traceableencoderlayer_pa_kernel(tc, x, ln1_w, qkv_w, out_0, out_1, out_
             stats = small.tile([P, DIM // BN_WIDTH, 6], F32)
             for s in range(DIM // BN_WIDTH):
                 nc.vector.bn_stats(out=stats[:, s, :], in_=x_rows[r][:, s * BN_WIDTH : (s + 1) * BN_WIDTH])
-            nc.vector.bn_aggr(out=mean_var[:, r, :], in_=stats[:].rearrange("p s f -> p (s f)"))
+                combine()
+            uncombined.append((r, stats))
+
+        def combine():
+            if uncombined:
+                slot, stats = uncombined.pop()
+                nc.vector.bn_aggr(out=mean_var[:, slot, :], in_=stats[:].rearrange("p s f -> p (s f)"))
 
         def normalise(r):
             from_scalar = r in SCALAR_STATS
@@ -173,6 +181,19 @@ def tile_traceableencoderlayer_pa_kernel(tc, x, ln1_w, qkv_w, out_0, out_1, out_
                 scale=1.0 / DIM if from_scalar else 1.0,
                 bias=EPS,
             )
+            z = stage.tile([P, PASSES, PACK, P], F32, name="z")
+            z_tiles[r] = z
+            x_parted = x_rows[r].rearrange("p (g w j) -> p g j w", w=P, j=PACK)
+            if r in VECTOR_NORM:
+                nc.vector.tensor_scalar(
+                    out=z[:],
+                    in0=x_parted,
+                    scalar1=minus_mean[:, r : r + 1] if from_scalar else mean_var[:, r, 0:1],
+                    scalar2=rstd[:, r : r + 1],
+                    op0=ALU.add if from_scalar else ALU.subtract,
+                    op1=ALU.mult,
+                )
+                return
             nc.gpsimd.tensor_scalar(
                 out=shift[:, r : r + 1],
                 in0=minus_mean[:, r : r + 1] if from_scalar else mean_var[:, r, 0:1],
@@ -181,16 +202,14 @@ def tile_traceableencoderlayer_pa_kernel(tc, x, ln1_w, qkv_w, out_0, out_1, out_
                 op0=ALU.mult,
                 op1=ALU.mult,
             )
-            z = stage.tile([P, PASSES, PACK, P], F32, name="z")
             nc.gpsimd.tensor_scalar(
                 out=z[:],
-                in0=x_rows[r].rearrange("p (g w j) -> p g j w", w=P, j=PACK),
+                in0=x_parted,
                 scalar1=rstd[:, r : r + 1],
                 scalar2=shift[:, r : r + 1],
                 op0=ALU.mult,
                 op1=ALU.add,
             )
-            z_tiles[r] = z
 
         def flip_tokens(r):
             for g in range(PASSES):
@@ -210,6 +229,7 @@ def tile_traceableencoderlayer_pa_kernel(tc, x, ln1_w, qkv_w, out_0, out_1, out_
                     in1=gain[:, g, :].unsqueeze(1).to_broadcast([P, P, PACK]),
                     op=ALU.mult,
                 )
+                combine()
 
         def quantise_tokens(r):
             nc.vector.quantize_mx(
@@ -255,8 +275,8 @@ def tile_traceableencoderlayer_pa_kernel(tc, x, ln1_w, qkv_w, out_0, out_1, out_
                 )
             w_grouped[c] = grouped
 
-        def quantise_weights(c):
-            for g in range(PASSES):
+        def quantise_weights(c, passes):
+            for g in passes:
                 nc.vector.quantize_mx(
                     out=w_codes[:, c, g, :].bitcast(FP8X4),
                     scales=w_scales[:, c, g, :],
@@ -277,7 +297,8 @@ def tile_traceableencoderlayer_pa_kernel(tc, x, ln1_w, qkv_w, out_0, out_1, out_
                 )
             products[c, r] = acc
 
-        def take_out(c, r, copy):
+        def take_out(c, r):
+            copy = nc.vector.tensor_copy if c >= LATE and (c * SLOTS + r) % 3 == 2 else nc.scalar.copy
             half, slot = divmod(r, HALF)
             if slot == 0:
                 result = res_pool.tile([P, CHUNK_HEADS, HALF, HEAD_DIM], F32, name="result")
@@ -312,41 +333,54 @@ def tile_traceableencoderlayer_pa_kernel(tc, x, ln1_w, qkv_w, out_0, out_1, out_
         ready_slots = []
         done = set()
         for i in range(len(ROUNDS)):
-            chunks, slots = ROUNDS[i]
+            chunks, slots, first, between = ROUNDS[i]
             units = [(c, r) for c in ready_chunks for r in ready_slots if (c, r) not in done]
+            for c, r in units[:first]:
+                multiply(c, r)
             for c in chunks:
                 flip_weights(c)
-            for r in slots:
+            for r in slots[:1]:
                 flip_tokens(r)
-            for c, r in units:
+            for c, r in units[first : first + between]:
                 multiply(c, r)
+            for r in slots[1:]:
+                flip_tokens(r)
+            for c, r in units[first + between :]:
+                multiply(c, r)
+            for c, r in units[:first]:
+                take_out(c, r)
             for c in chunks:
                 group_weights(c)
             to_normalise = [r + NORM_AHEAD for r in slots if r + NORM_AHEAD < SLOTS]
+            for r in slots:
+                if r + STATS_AHEAD < SLOTS and r + STATS_AHEAD not in SCALAR_STATS:
+                    statistics(r + STATS_AHEAD)
             for r in to_normalise:
                 if r in counted:
                     normalise(r)
             fresh = [r for r in to_normalise if r not in counted]
             for r in slots:
-                if r + STATS_AHEAD < SLOTS and r + STATS_AHEAD not in SCALAR_STATS:
-                    statistics(r + STATS_AHEAD)
                 if r + SCALAR_AHEAD in SCALAR_STATS:
                     statistics(r + SCALAR_AHEAD)
             for r in slots:
                 group_tokens(r)
+            for c in chunks:
+                quantise_weights(c, (0,))
             for r in slots[::2]:
                 quantise_tokens(r)
             for c in chunks:
-                quantise_weights(c)
+                quantise_weights(c, range(1, PASSES))
             for r in fresh:
                 normalise(r)
-            if i + SORT_AHEAD < len(ROUNDS):
-                for c in ROUNDS[i + SORT_AHEAD][0]:
-                    if c >= LATE:
-                        sort_weights(c)
-            for c, r in units:
-                late_third = c >= LATE and (c * SLOTS + r) % 3 == 2
-                take_out(c, r, nc.vector.tensor_copy if late_third else nc.scalar.copy)
+            to_sort = ROUNDS[i + SORT_AHEAD][0] if i + SORT_AHEAD < len(ROUNDS) else ()
+            for c in to_sort:
+                if c > LATE:
+                    sort_weights(c)
+            for c, r in units[first:]:
+                take_out(c, r)
+            for c in to_sort:
+                if c == LATE:
+                    sort_weights(c)
             for r in slots:
                 counted.add(r + STATS_AHEAD)
                 counted.add(r + SCALAR_AHEAD)

@@ -69,7 +69,7 @@ def tile_traceableencoderlayer_pa_kernel(tc, x, ln1_w, qkv_w, out_0, out_1, out_
         nc.vector.memset(gain_rows[:].bitcast(F32), 0.0)
 
         x_rows = {}
-        w_rows = qkv_w.rearrange("(c a p) k -> c p a k", a=ROW_BLOCKS, p=P)
+        w_rows = qkv_w.rearrange("(c p a) k -> c p a k", p=P, a=ROW_BLOCKS)
         w_raw = {}
         w_whole = {}
 
@@ -304,7 +304,10 @@ def tile_traceableencoderlayer_pa_kernel(tc, x, ln1_w, qkv_w, out_0, out_1, out_
                 result = res_pool.tile([P, CHUNK_HEADS, HALF, HEAD_DIM], F32, name="result")
                 results[c, half] = result
             result = results[c, half]
-            copy(out=result[:, :, slot, :], in_=products[c, r][:].rearrange("p (n d) -> p n d", d=HEAD_DIM))
+            copy(
+                out=result[:, :, slot, :].rearrange("p n (d a) -> p n d a", a=ROW_BLOCKS),
+                in_=products[c, r][:].rearrange("p (a n d) -> p n d a", a=ROW_BLOCKS, n=CHUNK_HEADS),
+            )
             if slot == HALF - 1:
                 store(c, half, 0, nc.sync)
                 if c < LATE:

@@ -31,22 +31,23 @@ BANKS = 2 * PASSES
 BN_WIDTH = 512
 
 ROUNDS = (
-    ((0,), (0, 1), 0, 0),
-    ((1,), (2, 3), 0, 0),
-    ((), (4, 5), 0, 0),
-    ((), (6, 7), 0, 2),
-    ((2,), (), 0, 0),
-    ((3,), (), 4, 0),
-    ((4,), (), 4, 0),
-    ((5,), (), 4, 0),
-    ((), (), 0, 0),
+    ((0,), (0, 1)),
+    ((1,), (2, 3)),
+    ((), (4, 5)),
+    ((), (6, 7)),
+    ((2,), ()),
+    ((3,), ()),
+    ((4,), ()),
+    ((5,), ()),
+    ((), ()),
 )
 LATE = 2
 STORE_LAG = 1
 SORT_AHEAD = 2
 SCALAR_STATS = (5, 7)
 SCALAR_AHEAD = 5
-VECTOR_NORM = (3, 5, 7)
+VECTOR_NORM = (1, 3, 6)
+SCALAR_NORM = (5,)
 STATS_AHEAD = 3
 NORM_AHEAD = 2
 
@@ -184,6 +185,16 @@ def tile_traceableencoderlayer_pa_kernel(tc, x, ln1_w, qkv_w, out_0, out_1, out_
             z = stage.tile([P, PASSES, PACK, P], F32, name="z")
             z_tiles[r] = z
             x_parted = x_rows[r].rearrange("p (g w j) -> p g j w", w=P, j=PACK)
+            if r in SCALAR_NORM:
+                if not from_scalar:
+                    nc.scalar.activation(out=minus_mean[:, r : r + 1], in_=mean_var[:, r, 0:1], func=ACT.Copy, scale=-1.0)
+                nc.scalar.activation(
+                    out=shift[:, r : r + 1], in_=minus_mean[:, r : r + 1], func=ACT.Copy, scale=rstd[:, r : r + 1]
+                )
+                nc.scalar.activation(
+                    out=z[:], in_=x_parted, func=ACT.Identity, scale=rstd[:, r : r + 1], bias=shift[:, r : r + 1]
+                )
+                return
             if r in VECTOR_NORM:
                 nc.vector.tensor_scalar(
                     out=z[:],
@@ -336,22 +347,14 @@ def tile_traceableencoderlayer_pa_kernel(tc, x, ln1_w, qkv_w, out_0, out_1, out_
         ready_slots = []
         done = set()
         for i in range(len(ROUNDS)):
-            chunks, slots, first, between = ROUNDS[i]
+            chunks, slots = ROUNDS[i]
             units = [(c, r) for c in ready_chunks for r in ready_slots if (c, r) not in done]
-            for c, r in units[:first]:
-                multiply(c, r)
             for c in chunks:
                 flip_weights(c)
-            for r in slots[:1]:
+            for r in slots:
                 flip_tokens(r)
-            for c, r in units[first : first + between]:
+            for c, r in units:
                 multiply(c, r)
-            for r in slots[1:]:
-                flip_tokens(r)
-            for c, r in units[first + between :]:
-                multiply(c, r)
-            for c, r in units[:first]:
-                take_out(c, r)
             for c in chunks:
                 group_weights(c)
             to_normalise = [r + NORM_AHEAD for r in slots if r + NORM_AHEAD < SLOTS]
@@ -379,7 +382,7 @@ def tile_traceableencoderlayer_pa_kernel(tc, x, ln1_w, qkv_w, out_0, out_1, out_
             for c in to_sort:
                 if c > LATE:
                     sort_weights(c)
-            for c, r in units[first:]:
+            for c, r in units:
                 take_out(c, r)
             for c in to_sort:
                 if c == LATE:

from contextlib import ExitStack

import concourse.mybir as mybir
from concourse.masks import make_identity

F32 = mybir.dt.float32
BF16 = mybir.dt.bfloat16
U32 = mybir.dt.uint32
U8 = mybir.dt.uint8
FP8X4 = mybir.dt.float8_e4m3fn_x4
ALU = mybir.AluOpType
ACT = mybir.ActivationFunctionType

P = 128
BATCH, SEQ, DIM = 4, 256, 1024
HEADS, HEAD_DIM = 16, 64
EPS = 1e-5

PACK = 4
K_PASS = P * PACK
PASSES = DIM // K_PASS
HALVES = 2
PAIR = BATCH // HALVES
HALF = PAIR * SEQ // P
SLOTS = HALVES * HALF
CHUNK = 512
CHUNK_HEADS = CHUNK // HEAD_DIM
CHUNKS = 3 * HEADS * HEAD_DIM // CHUNK
ROW_BLOCKS = CHUNK // P
BANKS = 2 * PASSES
BN_WIDTH = 512

ROUNDS = (
    ((0,), (0, 1)),
    ((1,), (2, 3)),
    ((), (4, 5)),
    ((), (6, 7)),
    ((2,), ()),
    ((3,), ()),
    ((4,), ()),
    ((5,), ()),
    ((), ()),
)
LATE = 2
STORE_LAG = 1
SORT_AHEAD = 2
SCALAR_STATS = (5, 7)
SCALAR_AHEAD = 5
VECTOR_NORM = (1, 3, 6)
SCALAR_NORM = (5,)
STATS_AHEAD = 3
NORM_AHEAD = 2

FLOPS = 2 * BATCH * SEQ * DIM * 3 * HEADS * HEAD_DIM


def tile_traceableencoderlayer_pa_kernel(tc, x, ln1_w, qkv_w, out_0, out_1, out_2):
    nc = tc.nc
    outs = (out_0, out_1, out_2)

    with ExitStack() as ctx:
        keep = ctx.enter_context(tc.tile_pool(name="keep", bufs=1))
        small = ctx.enter_context(tc.tile_pool(name="small", bufs=4))
        stage = ctx.enter_context(tc.tile_pool(name="stage", bufs=3))
        res_pool = ctx.enter_context(tc.tile_pool(name="res_pool", bufs=5))
        psum = ctx.enter_context(tc.psum_pool(name="psum", bufs=8))
        ctx.enter_context(tc.manual_schedule())

        gain_rows = keep.tile([P, K_PASS], BF16)
        nc.vector.memset(gain_rows[:].bitcast(F32), 0.0)

        x_rows = {}
        w_rows = qkv_w.rearrange("(c p a) k -> c p a k", p=P, a=ROW_BLOCKS)
        w_raw = {}
        w_whole = {}

        def load_tokens(first_slot, n_slots):
            half, r = divmod(first_slot, HALF)
            x_sb = keep.tile([P, n_slots, DIM], BF16, name="x_sb%d" % first_slot)
            for j in range(n_slots):
                x_rows[first_slot + j] = x_sb[:, j, :]
            for b in range(PAIR):
                nc.sync.dma_start(
                    out=x_sb[b:P:PAIR],
                    in_=x[PAIR * half + b].rearrange("(i r) k -> i r k", r=HALF)[:, r : r + n_slots, :],
                )

        def load_weights(c):
            pieces = 2 if c == 0 else 1
            blocks = ROW_BLOCKS // pieces
            for first in range(0, ROW_BLOCKS, blocks):
                raw = keep.tile([P, blocks, DIM], BF16, name="raw%d_%d" % (c, first))
                nc.sync.dma_start(out=raw[:], in_=w_rows[c][:, first : first + blocks, :])
                for a in range(blocks):
                    w_raw[c, first + a] = raw[:, a, :]
                w_whole[c] = raw

        load_tokens(0, 1)
        nc.sync.dma_start(out=gain_rows[0:PASSES, :], in_=ln1_w.rearrange("(r c) -> r c", c=K_PASS))
        load_tokens(1, 1)
        load_tokens(2, 2)
        load_weights(0)
        load_tokens(4, 2)
        load_tokens(6, 2)
        load_weights(1)
        for c in range(LATE, CHUNKS):
            load_weights(c)

        one = keep.tile([P, 1], F32)
        nc.vector.memset(one[:], 1.0)
        table_warmer = keep.tile([P, 1], F32)
        nc.scalar.activation(out=table_warmer[:], in_=one[:], func=ACT.Abs_reciprocal_sqrt)
        identity = keep.tile([P, P], F32)
        make_identity(nc, identity[:])

        gain_flip = psum.tile([P, PACK, P], F32, tag="bank")
        for u in range(2):
            nc.tensor.transpose(gain_flip[:, u, :], gain_rows[:].bitcast(F32)[:, u : 2 * P : 2], identity[:])
        gain_words = keep.tile([P, PASSES, 2], F32)
        nc.scalar.copy(out=gain_words[:], in_=gain_flip[:, 0:2, 0:PASSES].rearrange("p u g -> p g u"))
        gain = keep.tile([P, PASSES, PACK], F32)
        nc.scalar.copy(
            out=gain[:].rearrange("p g j -> p (g j)"),
            in_=gain_words[:].rearrange("p g u -> p (g u)").bitcast(BF16),
        )

        mean_var = keep.tile([P, SLOTS, 2], F32)
        rstd = keep.tile([P, SLOTS], F32)
        shift = keep.tile([P, SLOTS], F32)
        sums = keep.tile([P, SLOTS], F32)
        minus_mean = keep.tile([P, SLOTS], F32)
        squares = keep.tile([P, SLOTS], F32)
        h_codes = keep.tile([P, SLOTS, PASSES, P], U32, align_bytes=64)
        h_scales = keep.tile([P, SLOTS, PASSES, P], U8, align_bytes=64)
        w_codes = keep.tile([P, CHUNKS, PASSES, CHUNK], U32, align_bytes=64)
        w_scales = keep.tile([P, CHUNKS, PASSES, CHUNK], U8, align_bytes=64)
        z_tiles = {}
        z_flips = {}
        h_grouped = {}
        w_sorted = {}
        w_flips = {}
        w_grouped = {}
        products = {}
        waiting = []
        results = {}
        uncombined = []

        def statistics(r):
            if r in SCALAR_STATS:
                unused = stage.tile([P, DIM], BF16, name="unused")
                nc.scalar.activation(
                    out=unused[:], in_=x_rows[r], func=ACT.Identity, accum_out=sums[:, r : r + 1]
                )
                nc.scalar.activation(
                    out=minus_mean[:, r : r + 1], in_=sums[:, r : r + 1], func=ACT.Copy, scale=-1.0 / DIM
                )
                nc.scalar.activation(
                    out=unused[:],
                    in_=x_rows[r],
                    func=ACT.Square,
                    bias=minus_mean[:, r : r + 1],
                    accum_out=squares[:, r : r + 1],
                )
                return
            stats = small.tile([P, DIM // BN_WIDTH, 6], F32)
            for s in range(DIM // BN_WIDTH):
                nc.vector.bn_stats(out=stats[:, s, :], in_=x_rows[r][:, s * BN_WIDTH : (s + 1) * BN_WIDTH])
                combine()
            uncombined.append((r, stats))

        def combine():
            if uncombined:
                slot, stats = uncombined.pop()
                nc.vector.bn_aggr(out=mean_var[:, slot, :], in_=stats[:].rearrange("p s f -> p (s f)"))

        def normalise(r):
            from_scalar = r in SCALAR_STATS
            nc.scalar.activation(
                out=rstd[:, r : r + 1],
                in_=squares[:, r : r + 1] if from_scalar else mean_var[:, r, 1:2],
                func=ACT.Abs_reciprocal_sqrt,
                scale=1.0 / DIM if from_scalar else 1.0,
                bias=EPS,
            )
            z = stage.tile([P, PASSES, PACK, P], F32, name="z")
            z_tiles[r] = z
            x_parted = x_rows[r].rearrange("p (g w j) -> p g j w", w=P, j=PACK)
            if r in SCALAR_NORM:
                if not from_scalar:
                    nc.scalar.activation(out=minus_mean[:, r : r + 1], in_=mean_var[:, r, 0:1], func=ACT.Copy, scale=-1.0)
                nc.scalar.activation(
                    out=shift[:, r : r + 1], in_=minus_mean[:, r : r + 1], func=ACT.Copy, scale=rstd[:, r : r + 1]
                )
                nc.scalar.activation(
                    out=z[:], in_=x_parted, func=ACT.Identity, scale=rstd[:, r : r + 1], bias=shift[:, r : r + 1]
                )
                return
            if r in VECTOR_NORM:
                nc.vector.tensor_scalar(
                    out=z[:],
                    in0=x_parted,
                    scalar1=minus_mean[:, r : r + 1] if from_scalar else mean_var[:, r, 0:1],
                    scalar2=rstd[:, r : r + 1],
                    op0=ALU.add if from_scalar else ALU.subtract,
                    op1=ALU.mult,
                )
                return
            nc.gpsimd.tensor_scalar(
                out=shift[:, r : r + 1],
                in0=minus_mean[:, r : r + 1] if from_scalar else mean_var[:, r, 0:1],
                scalar1=rstd[:, r : r + 1],
                scalar2=1.0 if from_scalar else -1.0,
                op0=ALU.mult,
                op1=ALU.mult,
            )
            nc.gpsimd.tensor_scalar(
                out=z[:],
                in0=x_parted,
                scalar1=rstd[:, r : r + 1],
                scalar2=shift[:, r : r + 1],
                op0=ALU.mult,
                op1=ALU.add,
            )

        def flip_tokens(r):
            for g in range(PASSES):
                flip = psum.tile([P, PACK, P], F32, tag="bank")
                for j in range(PACK):
                    nc.tensor.transpose(flip[:, j, :], z_tiles[r][:, g, j, :], identity[:])
                z_flips[r, g] = flip

        def group_tokens(r):
            if r % 2 == 0:
                pair = stage.tile([P, 2, PASSES, P, PACK], BF16, name="pair", align_bytes=64)
                h_grouped[r] = pair
            for g in range(PASSES):
                nc.vector.tensor_tensor(
                    out=h_grouped[r - r % 2][:, r % 2, g, :, :],
                    in0=z_flips[r, g][:].rearrange("p j i -> p i j"),
                    in1=gain[:, g, :].unsqueeze(1).to_broadcast([P, P, PACK]),
                    op=ALU.mult,
                )
                combine()

        def quantise_tokens(r):
            nc.vector.quantize_mx(
                out=h_codes[:, r : r + 2].rearrange("p s g i -> p (s g i)").bitcast(FP8X4),
                scales=h_scales[:, r : r + 2].rearrange("p s g i -> p (s g i)"),
                in_=h_grouped[r][:].rearrange("p s g i j -> p (s g i j)"),
            )

        def sort_weights(c):
            sorted_words = stage.tile([P, ROW_BLOCKS, 2, DIM // PACK], F32, name="sorted_words")
            copy = nc.scalar.copy if c == LATE else nc.vector.tensor_copy
            copy(
                out=sorted_words[:], in_=w_whole[c][:].bitcast(F32).rearrange("p a (q u) -> p a u q", u=2)
            )
            w_sorted[c] = sorted_words

        def bank_order(c):
            if c == 0:
                return [(g, pair) for pair in range(2) for g in range(PASSES)]
            return [(g, pair) for g in range(PASSES) for pair in range(2)]

        def flip_weights(c):
            for g, pair in bank_order(c):
                flip = psum.tile([P, 2, 2, P], F32, tag="bank")
                for u in range(2):
                    for a in range(2):
                        block = 2 * pair + a
                        if c in w_sorted:
                            source = w_sorted[c][:, block, u, g * P : (g + 1) * P]
                        else:
                            source = w_raw[c, block].bitcast(F32)[:, 2 * P * g + u : 2 * P * (g + 1) : 2]
                        nc.tensor.transpose(flip[:, u, a, :], source, identity[:])
                w_flips[c, g, pair] = flip

        def group_weights(c):
            grouped = stage.tile([P, PASSES, CHUNK, PACK], BF16, name="w_grouped", align_bytes=64)
            grouped_words = grouped[:].bitcast(F32)
            for g, pair in bank_order(c):
                copy = nc.vector.tensor_copy if c >= LATE and pair == 1 else nc.scalar.copy
                copy(
                    out=grouped_words[:, g, 2 * pair * P : (2 * pair + 2) * P, :],
                    in_=w_flips[c, g, pair][:].rearrange("p u a n -> p (a n) u"),
                )
            w_grouped[c] = grouped

        def quantise_weights(c, passes):
            for g in passes:
                nc.vector.quantize_mx(
                    out=w_codes[:, c, g, :].bitcast(FP8X4),
                    scales=w_scales[:, c, g, :],
                    in_=w_grouped[c][:, g, :, :].rearrange("p n j -> p (n j)"),
                )

        def multiply(c, r):
            acc = psum.tile([P, CHUNK], F32, tag="bank")
            for g in range(PASSES):
                nc.tensor.matmul_mx(
                    out=acc[:],
                    lhsT=h_codes[:, r, g, :].bitcast(FP8X4),
                    lhsT_scale=h_scales[:, r, g, :],
                    rhs=w_codes[:, c, g, :].bitcast(FP8X4),
                    rhs_scale=w_scales[:, c, g, :],
                    start=(g == 0),
                    stop=(g == PASSES - 1),
                )
            products[c, r] = acc

        def take_out(c, r):
            copy = nc.vector.tensor_copy if c >= LATE and (c * SLOTS + r) % 3 == 2 else nc.scalar.copy
            half, slot = divmod(r, HALF)
            if slot == 0:
                result = res_pool.tile([P, CHUNK_HEADS, HALF, HEAD_DIM], F32, name="result")
                results[c, half] = result
            result = results[c, half]
            copy(
                out=result[:, :, slot, :].rearrange("p n (d a) -> p n d a", a=ROW_BLOCKS),
                in_=products[c, r][:].rearrange("p (a n d) -> p n d a", a=ROW_BLOCKS, n=CHUNK_HEADS),
            )
            if slot == HALF - 1:
                store(c, half, 0, nc.sync)
                if c < LATE:
                    store(c, half, 1, nc.sync)
                else:
                    waiting.append((c, half))
            if waiting and slot == STORE_LAG:
                store(*waiting.pop(0), 1, nc.scalar)

        def store(c, half, b, queue):
            which, first_head = divmod(c * CHUNK_HEADS, HEADS)
            queue.dma_start(
                out=outs[which][PAIR * half + b, first_head : first_head + CHUNK_HEADS].rearrange(
                    "n (i r) d -> i n r d", r=HALF
                ),
                in_=results[c, half][b:P:PAIR],
            )

        for r in range(STATS_AHEAD):
            statistics(r)
            if r > 0:
                normalise(r - 1)

        counted = set(range(STATS_AHEAD))
        ready_chunks = []
        ready_slots = []
        done = set()
        for i in range(len(ROUNDS)):
            chunks, slots = ROUNDS[i]
            units = [(c, r) for c in ready_chunks for r in ready_slots if (c, r) not in done]
            for c in chunks:
                flip_weights(c)
            for r in slots:
                flip_tokens(r)
            for c, r in units:
                multiply(c, r)
            for c in chunks:
                group_weights(c)
            to_normalise = [r + NORM_AHEAD for r in slots if r + NORM_AHEAD < SLOTS]
            for r in slots:
                if r + STATS_AHEAD < SLOTS and r + STATS_AHEAD not in SCALAR_STATS:
                    statistics(r + STATS_AHEAD)
            for r in to_normalise:
                if r in counted:
                    normalise(r)
            fresh = [r for r in to_normalise if r not in counted]
            for r in slots:
                if r + SCALAR_AHEAD in SCALAR_STATS:
                    statistics(r + SCALAR_AHEAD)
            for r in slots:
                group_tokens(r)
            for c in chunks:
                quantise_weights(c, (0,))
            for r in slots[::2]:
                quantise_tokens(r)
            for c in chunks:
                quantise_weights(c, range(1, PASSES))
            for r in fresh:
                normalise(r)
            to_sort = ROUNDS[i + SORT_AHEAD][0] if i + SORT_AHEAD < len(ROUNDS) else ()
            for c in to_sort:
                if c > LATE:
                    sort_weights(c)
            for c, r in units:
                take_out(c, r)
            for c in to_sort:
                if c == LATE:
                    sort_weights(c)
            for r in slots:
                counted.add(r + STATS_AHEAD)
                counted.add(r + SCALAR_AHEAD)
            if i == len(ROUNDS) - 1:
                for c, half in waiting:
                    store(c, half, 1, nc.scalar)
            for u in units:
                done.add(u)
            ready_chunks.extend(chunks)
            ready_slots.extend(slots)
